import numpy as np
import ml_dtypes


def mxq(x, axis, fmt="e4m3"):
    dtype, down = {"e4m3": (ml_dtypes.float8_e4m3fn, 7), "e5m2": (ml_dtypes.float8_e5m2, 14)}[fmt]
    v = np.moveaxis(np.asarray(x, np.float32).astype(ml_dtypes.bfloat16).astype(np.float64), axis, -1)
    blocks = v.reshape(v.shape[:-1] + (-1, 32))
    amax = np.abs(blocks).max(-1, keepdims=True)
    byte = np.maximum(np.where(amax > 0, np.frexp(amax)[1] - 1 + 127, 0) - down, 1)
    scale = np.exp2(byte - 127.0)
    codes = (blocks / scale).astype(np.float32).astype(dtype).astype(np.float64)
    return np.moveaxis((codes * scale).reshape(v.shape), -1, axis)


WIDE = False


def mx_kscale(k):
    if not WIDE:
        return np.ones(k)
    levels = np.array([10, -10, 5, -5, 0])
    a = np.random.permutation(np.resize(levels, k // 512 * 4)).reshape(k // 512, 4)
    idx = np.arange(k)
    return np.exp2(a[idx // 512, idx % 128 // 32])


BF16 = ml_dtypes.bfloat16


def bf(x):
    return np.asarray(x, np.float32).astype(BF16)


def f64(x):
    return np.asarray(x).astype(np.float64)


B, S, H, R = 2, 512, 4096, 1024
G = H // R


def setup_inputs():
    s = mx_kscale(R)
    return {"x": bf(np.random.standard_normal((B, S, H)) * np.tile(s, G)),
            "matrix": bf(np.random.standard_normal((R, R)) / np.sqrt(R) / s[:, None])}


def reference(x, matrix):
    x, matrix = f64(x), f64(matrix)
    b, n, h = x.shape
    r = matrix.shape[0]
    g = h // r
    compressed = x.reshape(b, n, g, r).sum(axis=2)
    out = mxq(compressed, 2, "e4m3") @ mxq(matrix, 0, "e4m3")
    return np.repeat(out, g, axis=2)[:, :, :h]

@@ -1,0 +1,159 @@
+from contextlib import ExitStack
+
+import concourse.mybir as mybir
+from concourse.masks import make_identity
+
+BF16 = mybir.dt.bfloat16
+F32 = mybir.dt.float32
+U32 = mybir.dt.uint32
+U8 = mybir.dt.uint8
+FP8X4 = mybir.dt.float8_e4m3fn_x4
+ADD = mybir.AluOpType.add
+
+P = 128
+TOKENS = 1024
+H = 4096
+R = 1024
+G = 4
+NT = TOKENS // P
+PASSES = R // 512
+NH = R // 512
+
+FLOPS = 2 * TOKENS * R * R
+
+VECTOR_EXITS = ((1, 1), (4, 1), (6, 1))
+X_CHUNKS = ((0, 1), (1, 2), (2, 4), (4, 8))
+
+
+def tile_mora_kernel(tc, x, matrix, out):
+    nc = tc.nc
+    x_v = x.flatten_outer_dims().rearrange("(p t) h -> p t h", t=NT)
+    out_v = out.flatten_outer_dims().rearrange("(p t) h -> p t h", t=NT)
+    m_v = matrix.rearrange("(g t p) n -> g p t n", t=4, p=P)
+
+    with ExitStack() as ctx:
+        keep = ctx.enter_context(tc.tile_pool(name="keep", bufs=1))
+        work = ctx.enter_context(tc.tile_pool(name="work", bufs=2))
+        stage = ctx.enter_context(tc.tile_pool(name="stage", bufs=5))
+        psum_t = ctx.enter_context(tc.psum_pool(name="psum_t", bufs=2))
+        psum_y = ctx.enter_context(tc.psum_pool(name="psum_y", bufs=6))
+
+        ident = keep.tile([P, P], BF16, name="ident")
+        make_identity(nc, ident[:])
+
+        x_tiles = {}
+        m_raw = []
+
+        def load_x(chunk):
+            lo, hi = X_CHUNKS[chunk]
+            xt = keep.tile([P, hi - lo, H], BF16, name="x%d" % chunk)
+            nc.sync.dma_start(out=xt[:], in_=x_v[:, lo:hi, :])
+            for t in range(lo, hi):
+                x_tiles[t] = xt[:, t - lo, :]
+
+        def load_m(g):
+            mr = keep.tile([P, 4, R], BF16, name="mraw%d" % g)
+            nc.sync.dma_start(out=mr[:], in_=m_v[g])
+            m_raw.append(mr)
+
+        load_x(0)
+        load_m(0)
+        load_m(1)
+        load_x(1)
+        load_x(2)
+        load_x(3)
+
+        c_tiles = {}
+        cq = {}
+
+        def compress(t):
+            xv = x_tiles[t].rearrange("p (a b i) -> p a b i", a=2, b=2)
+            s = work.tile([P, 2, R], F32, name="s")
+            nc.vector.tensor_tensor(out=s[:], in0=xv[:, :, 0, :], in1=xv[:, :, 1, :], op=ADD)
+            c = work.tile([P, R], BF16, name="c")
+            nc.vector.tensor_tensor(out=c[:], in0=s[:, 0, :], in1=s[:, 1, :], op=ADD)
+            c_tiles[t] = c
+
+        def turn(t):
+            c = c_tiles[t]
+            tp = psum_t.tile([P, 2 * 4, P], BF16, name="tp")
+            for b in range(8):
+                nc.tensor.transpose(tp[:, b, :], c[:, P * b : P * (b + 1)], ident[:])
+            cg = work.tile([P, PASSES, P, 4], BF16, name="cg", align_bytes=64)
+            nc.scalar.copy(out=cg[:], in_=tp[:].rearrange("p (g t) r -> p g r t", t=4))
+            c_tiles[t] = cg
+
+        def quantise_c(t):
+            cg = c_tiles[t]
+            codes = work.tile([P, PASSES * P], U32, name="ccodes", align_bytes=64)
+            scales = work.tile([P, PASSES * P], U8, name="cscales", align_bytes=64)
+            nc.vector.quantize_mx(
+                out=codes[:].bitcast(FP8X4),
+                scales=scales[:],
+                in_=cg[:].rearrange("p g r t -> p (g r t)"),
+            )
+            cq[t] = (codes, scales)
+
+        m_q = {}
+        m_grouped = {}
+
+        def regroup_m(g, h, engine):
+            mg = keep.tile([P, 512, 4], BF16, name="mg%d%d" % (g, h), align_bytes=64)
+            src = m_raw[g][:, :, 512 * h : 512 * (h + 1)].rearrange("p t (c i) -> p c t i", i=4)
+            dst = mg[:].rearrange("p (c i) t -> p c t i", i=4)
+            if engine == "v":
+                nc.vector.tensor_copy(out=dst, in_=src)
+            else:
+                nc.scalar.copy(out=dst, in_=src)
+            m_grouped[(g, h)] = mg
+
+        def quantise_m(g, h):
+            codes = keep.tile([P, 512], U32, name="mcodes%d%d" % (g, h), align_bytes=64)
+            scales = keep.tile([P, 512], U8, name="mscales%d%d" % (g, h), align_bytes=64)
+            nc.vector.quantize_mx(
+                out=codes[:].bitcast(FP8X4),
+                scales=scales[:],
+                in_=m_grouped[(g, h)][:].rearrange("p n t -> p (n t)"),
+            )
+            m_q[(g, h)] = (codes, scales)
+
+        def multiply(t):
+            codes, scales = cq[t]
+            o = stage.tile([P, H], F32, name="o")
+            for h in range(NH):
+                y = psum_y.tile([P, 512], F32, name="y")
+                for g in range(PASSES):
+                    mc, ms = m_q[(g, h)]
+                    nc.tensor.matmul_mx(
+                        out=y[:],
+                        lhsT=codes[:, P * g : P * (g + 1)].bitcast(FP8X4),
+                        lhsT_scale=scales[:, P * g : P * (g + 1)],
+                        rhs=mc[:].bitcast(FP8X4),
+                        rhs_scale=ms[:],
+                        start=(g == 0),
+                        stop=(g == PASSES - 1),
+                    )
+                dst = o[:, 2048 * h : 2048 * (h + 1)].rearrange("p (n j) -> p n j", j=G)
+                src = y[:].unsqueeze(2).to_broadcast([P, 512, G])
+                if (t, h) in VECTOR_EXITS:
+                    nc.vector.tensor_copy(out=dst, in_=src)
+                else:
+                    nc.scalar.copy(out=dst, in_=src)
+            nc.sync.dma_start(out=out_v[:, t, :], in_=o[:])
+
+        compress(0)
+        regroup_m(0, 0, "s")
+        regroup_m(1, 0, "v")
+        regroup_m(0, 1, "v")
+        regroup_m(1, 1, "s")
+        turn(0)
+        quantise_m(0, 0)
+        quantise_m(1, 0)
+        quantise_m(0, 1)
+        quantise_m(1, 1)
+        for t in range(NT):
+            if t + 1 < NT:
+                compress(t + 1)
+                turn(t + 1)
+            quantise_c(t)
+            multiply(t)

@@ -21,8 +21,8 @@ NH = R // 512
 
 FLOPS = 2 * TOKENS * R * R
 
-VECTOR_EXITS = ((1, 1), (4, 1), (6, 1))
-X_CHUNKS = ((0, 1), (1, 2), (2, 4), (4, 8))
+VECTOR_EXITS = ((2, 1), (3, 1), (4, 1), (5, 1), (6, 1), (7, 1))
+X_CHUNKS = ((0, 1), (1, 2), (2, 4), (4, 6), (6, 8))
 
 
 def tile_mora_kernel(tc, x, matrix, out):
@@ -35,10 +35,10 @@ def tile_mora_kernel(tc, x, matrix, out):
         keep = ctx.enter_context(tc.tile_pool(name="keep", bufs=1))
         work = ctx.enter_context(tc.tile_pool(name="work", bufs=2))
         stage = ctx.enter_context(tc.tile_pool(name="stage", bufs=5))
-        psum_t = ctx.enter_context(tc.psum_pool(name="psum_t", bufs=2))
-        psum_y = ctx.enter_context(tc.psum_pool(name="psum_y", bufs=6))
+        psum_t = ctx.enter_context(tc.psum_pool(name="psum_t", bufs=4))
+        psum_y = ctx.enter_context(tc.psum_pool(name="psum_y", bufs=4))
 
-        ident = keep.tile([P, P], BF16, name="ident")
+        ident = keep.tile([P, P], F32, name="ident")
         make_identity(nc, ident[:])
 
         x_tiles = {}
@@ -62,35 +62,52 @@ def tile_mora_kernel(tc, x, matrix, out):
         load_x(1)
         load_x(2)
         load_x(3)
+        load_x(4)
 
-        c_tiles = {}
+        sums = {}
+        turned = {}
+        grouped = {}
         cq = {}
 
         def compress(t):
             xv = x_tiles[t].rearrange("p (a b i) -> p a b i", a=2, b=2)
             s = work.tile([P, 2, R], F32, name="s")
             nc.vector.tensor_tensor(out=s[:], in0=xv[:, :, 0, :], in1=xv[:, :, 1, :], op=ADD)
-            c = work.tile([P, R], BF16, name="c")
-            nc.vector.tensor_tensor(out=c[:], in0=s[:, 0, :], in1=s[:, 1, :], op=ADD)
-            c_tiles[t] = c
+            sums[t] = s
 
         def turn(t):
-            c = c_tiles[t]
-            tp = psum_t.tile([P, 2 * 4, P], BF16, name="tp")
-            for b in range(8):
-                nc.tensor.transpose(tp[:, b, :], c[:, P * b : P * (b + 1)], ident[:])
+            s = sums[t]
+            banks = []
+            for g in range(PASSES):
+                tp = psum_t.tile([P, 4, P], F32, name="tp")
+                for u in range(4):
+                    b = 4 * g + u
+                    for a in range(2):
+                        nc.tensor.matmul(
+                            out=tp[:, u, :],
+                            lhsT=s[:, a, P * b : P * (b + 1)],
+                            rhs=ident[:],
+                            is_transpose=True,
+                            start=(a == 0),
+                            stop=(a == 1),
+                        )
+                banks.append(tp)
+            turned[t] = banks
+
+        def regroup_c(t):
             cg = work.tile([P, PASSES, P, 4], BF16, name="cg", align_bytes=64)
-            nc.scalar.copy(out=cg[:], in_=tp[:].rearrange("p (g t) r -> p g r t", t=4))
-            c_tiles[t] = cg
+            for g in range(PASSES):
+                nc.scalar.copy(out=cg[:, g], in_=turned[t][g][:].rearrange("p u r -> p r u"))
+            grouped[t] = cg
 
         def quantise_c(t):
-            cg = c_tiles[t]
+            cg = grouped[t]
             codes = work.tile([P, PASSES * P], U32, name="ccodes", align_bytes=64)
             scales = work.tile([P, PASSES * P], U8, name="cscales", align_bytes=64)
             nc.vector.quantize_mx(
                 out=codes[:].bitcast(FP8X4),
                 scales=scales[:],
-                in_=cg[:].rearrange("p g r t -> p (g r t)"),
+                in_=cg[:].rearrange("p g r u -> p (g r u)"),
             )
             cq[t] = (codes, scales)
 
@@ -117,9 +134,11 @@ def tile_mora_kernel(tc, x, matrix, out):
             )
             m_q[(g, h)] = (codes, scales)
 
+        products = {}
+
         def multiply(t):
             codes, scales = cq[t]
-            o = stage.tile([P, H], F32, name="o")
+            banks = []
             for h in range(NH):
                 y = psum_y.tile([P, 512], F32, name="y")
                 for g in range(PASSES):
@@ -133,8 +152,14 @@ def tile_mora_kernel(tc, x, matrix, out):
                         start=(g == 0),
                         stop=(g == PASSES - 1),
                     )
+                banks.append(y)
+            products[t] = banks
+
+        def decompress(t):
+            o = stage.tile([P, H], F32, name="o")
+            for h in range(NH):
                 dst = o[:, 2048 * h : 2048 * (h + 1)].rearrange("p (n j) -> p n j", j=G)
-                src = y[:].unsqueeze(2).to_broadcast([P, 512, G])
+                src = products[t][h][:].unsqueeze(2).to_broadcast([P, 512, G])
                 if (t, h) in VECTOR_EXITS:
                     nc.vector.tensor_copy(out=dst, in_=src)
                 else:
@@ -142,18 +167,26 @@ def tile_mora_kernel(tc, x, matrix, out):
             nc.sync.dma_start(out=out_v[:, t, :], in_=o[:])
 
         compress(0)
-        regroup_m(0, 0, "s")
-        regroup_m(1, 0, "v")
-        regroup_m(0, 1, "v")
-        regroup_m(1, 1, "s")
         turn(0)
+        regroup_m(0, 0, "v")
+        regroup_m(0, 1, "s")
+        regroup_c(0)
+        regroup_m(1, 0, "v")
+        regroup_m(1, 1, "s")
         quantise_m(0, 0)
         quantise_m(1, 0)
+        quantise_c(0)
         quantise_m(0, 1)
         quantise_m(1, 1)
+        multiply(0)
+        compress(1)
+        turn(1)
         for t in range(NT):
+            if t + 2 < NT:
+                compress(t + 2)
+                turn(t + 2)
             if t + 1 < NT:
-                compress(t + 1)
-                turn(t + 1)
-            quantise_c(t)
-            multiply(t)
+                regroup_c(t + 1)
+                quantise_c(t + 1)
+                multiply(t + 1)
+            decompress(t)

@@ -29,7 +29,7 @@ def tile_mora_kernel(tc, x, matrix, out):
     nc = tc.nc
     x_v = x.flatten_outer_dims().rearrange("(p t) h -> p t h", t=NT)
     out_v = out.flatten_outer_dims().rearrange("(p t) h -> p t h", t=NT)
-    m_v = matrix.rearrange("(g t p) n -> g p t n", t=4, p=P)
+    m_v = matrix.rearrange("(g p t) n -> g p t n", t=4, p=P)
 
     with ExitStack() as ctx:
         keep = ctx.enter_context(tc.tile_pool(name="keep", bufs=1))
@@ -76,16 +76,15 @@ def tile_mora_kernel(tc, x, matrix, out):
             sums[t] = s
 
         def turn(t):
-            s = sums[t]
+            s = sums[t][:].rearrange("p a (g q u) -> p a g u q", g=PASSES, u=4)
             banks = []
             for g in range(PASSES):
                 tp = psum_t.tile([P, 4, P], F32, name="tp")
                 for u in range(4):
-                    b = 4 * g + u
                     for a in range(2):
                         nc.tensor.matmul(
                             out=tp[:, u, :],
-                            lhsT=s[:, a, P * b : P * (b + 1)],
+                            lhsT=s[:, a, g, u, :],
                             rhs=ident[:],
                             is_transpose=True,
                             start=(a == 0),

from contextlib import ExitStack

import concourse.mybir as mybir
from concourse.masks import make_identity

BF16 = mybir.dt.bfloat16
F32 = mybir.dt.float32
U32 = mybir.dt.uint32
U8 = mybir.dt.uint8
FP8X4 = mybir.dt.float8_e4m3fn_x4
ADD = mybir.AluOpType.add

P = 128
TOKENS = 1024
H = 4096
R = 1024
G = 4
NT = TOKENS // P
PASSES = R // 512
NH = R // 512

FLOPS = 2 * TOKENS * R * R

VECTOR_EXITS = ((2, 1), (3, 1), (4, 1), (5, 1), (6, 1), (7, 1))
X_CHUNKS = ((0, 1), (1, 2), (2, 4), (4, 6), (6, 8))


def tile_mora_kernel(tc, x, matrix, out):
    nc = tc.nc
    x_v = x.flatten_outer_dims().rearrange("(p t) h -> p t h", t=NT)
    out_v = out.flatten_outer_dims().rearrange("(p t) h -> p t h", t=NT)
    m_v = matrix.rearrange("(g p t) n -> g p t n", t=4, p=P)

    with ExitStack() as ctx:
        keep = ctx.enter_context(tc.tile_pool(name="keep", bufs=1))
        work = ctx.enter_context(tc.tile_pool(name="work", bufs=2))
        stage = ctx.enter_context(tc.tile_pool(name="stage", bufs=5))
        psum_t = ctx.enter_context(tc.psum_pool(name="psum_t", bufs=4))
        psum_y = ctx.enter_context(tc.psum_pool(name="psum_y", bufs=4))

        ident = keep.tile([P, P], F32, name="ident")
        make_identity(nc, ident[:])

        x_tiles = {}
        m_raw = []

        def load_x(chunk):
            lo, hi = X_CHUNKS[chunk]
            xt = keep.tile([P, hi - lo, H], BF16, name="x%d" % chunk)
            nc.sync.dma_start(out=xt[:], in_=x_v[:, lo:hi, :])
            for t in range(lo, hi):
                x_tiles[t] = xt[:, t - lo, :]

        def load_m(g):
            mr = keep.tile([P, 4, R], BF16, name="mraw%d" % g)
            nc.sync.dma_start(out=mr[:], in_=m_v[g])
            m_raw.append(mr)

        load_x(0)
        load_m(0)
        load_m(1)
        load_x(1)
        load_x(2)
        load_x(3)
        load_x(4)

        sums = {}
        turned = {}
        grouped = {}
        cq = {}

        def compress(t):
            xv = x_tiles[t].rearrange("p (a b i) -> p a b i", a=2, b=2)
            s = work.tile([P, 2, R], F32, name="s")
            nc.vector.tensor_tensor(out=s[:], in0=xv[:, :, 0, :], in1=xv[:, :, 1, :], op=ADD)
            sums[t] = s

        def turn(t):
            s = sums[t][:].rearrange("p a (g q u) -> p a g u q", g=PASSES, u=4)
            banks = []
            for g in range(PASSES):
                tp = psum_t.tile([P, 4, P], F32, name="tp")
                for u in range(4):
                    for a in range(2):
                        nc.tensor.matmul(
                            out=tp[:, u, :],
                            lhsT=s[:, a, g, u, :],
                            rhs=ident[:],
                            is_transpose=True,
                            start=(a == 0),
                            stop=(a == 1),
                        )
                banks.append(tp)
            turned[t] = banks

        def regroup_c(t):
            cg = work.tile([P, PASSES, P, 4], BF16, name="cg", align_bytes=64)
            for g in range(PASSES):
                nc.scalar.copy(out=cg[:, g], in_=turned[t][g][:].rearrange("p u r -> p r u"))
            grouped[t] = cg

        def quantise_c(t):
            cg = grouped[t]
            codes = work.tile([P, PASSES * P], U32, name="ccodes", align_bytes=64)
            scales = work.tile([P, PASSES * P], U8, name="cscales", align_bytes=64)
            nc.vector.quantize_mx(
                out=codes[:].bitcast(FP8X4),
                scales=scales[:],
                in_=cg[:].rearrange("p g r u -> p (g r u)"),
            )
            cq[t] = (codes, scales)

        m_q = {}
        m_grouped = {}

        def regroup_m(g, h, engine):
            mg = keep.tile([P, 512, 4], BF16, name="mg%d%d" % (g, h), align_bytes=64)
            src = m_raw[g][:, :, 512 * h : 512 * (h + 1)].rearrange("p t (c i) -> p c t i", i=4)
            dst = mg[:].rearrange("p (c i) t -> p c t i", i=4)
            if engine == "v":
                nc.vector.tensor_copy(out=dst, in_=src)
            else:
                nc.scalar.copy(out=dst, in_=src)
            m_grouped[(g, h)] = mg

        def quantise_m(g, h):
            codes = keep.tile([P, 512], U32, name="mcodes%d%d" % (g, h), align_bytes=64)
            scales = keep.tile([P, 512], U8, name="mscales%d%d" % (g, h), align_bytes=64)
            nc.vector.quantize_mx(
                out=codes[:].bitcast(FP8X4),
                scales=scales[:],
                in_=m_grouped[(g, h)][:].rearrange("p n t -> p (n t)"),
            )
            m_q[(g, h)] = (codes, scales)

        products = {}

        def multiply(t):
            codes, scales = cq[t]
            banks = []
            for h in range(NH):
                y = psum_y.tile([P, 512], F32, name="y")
                for g in range(PASSES):
                    mc, ms = m_q[(g, h)]
                    nc.tensor.matmul_mx(
                        out=y[:],
                        lhsT=codes[:, P * g : P * (g + 1)].bitcast(FP8X4),
                        lhsT_scale=scales[:, P * g : P * (g + 1)],
                        rhs=mc[:].bitcast(FP8X4),
                        rhs_scale=ms[:],
                        start=(g == 0),
                        stop=(g == PASSES - 1),
                    )
                banks.append(y)
            products[t] = banks

        def decompress(t):
            o = stage.tile([P, H], F32, name="o")
            for h in range(NH):
                dst = o[:, 2048 * h : 2048 * (h + 1)].rearrange("p (n j) -> p n j", j=G)
                src = products[t][h][:].unsqueeze(2).to_broadcast([P, 512, G])
                if (t, h) in VECTOR_EXITS:
                    nc.vector.tensor_copy(out=dst, in_=src)
                else:
                    nc.scalar.copy(out=dst, in_=src)
            nc.sync.dma_start(out=out_v[:, t, :], in_=o[:])

        compress(0)
        turn(0)
        regroup_m(0, 0, "v")
        regroup_m(0, 1, "s")
        regroup_c(0)
        regroup_m(1, 0, "v")
        regroup_m(1, 1, "s")
        quantise_m(0, 0)
        quantise_m(1, 0)
        quantise_c(0)
        quantise_m(0, 1)
        quantise_m(1, 1)
        multiply(0)
        compress(1)
        turn(1)
        for t in range(NT):
            if t + 2 < NT:
                compress(t + 2)
                turn(t + 2)
            if t + 1 < NT:
                regroup_c(t + 1)
                quantise_c(t + 1)
                multiply(t + 1)
            decompress(t)
